import numpy as np
import ml_dtypes

BF16 = ml_dtypes.bfloat16


def bf(x):
    return np.asarray(x, np.float32).astype(BF16)


def f32(x):
    return np.asarray(x, np.float32)


def f64(x):
    return np.asarray(x).astype(np.float64)


def striped(idx):
    return np.tile(idx.reshape(-1, 16).T, (8, 1))


C, S, K, P, N = 128, 1024, 4, 512, 2048


def setup_inputs():
    x = f32(np.random.uniform(0.5, 4.0, (1, S)) * np.random.uniform(0.0, 1.0, (C, S)))
    ff = f32(np.random.uniform(0.5, 4.0, (1, P)) * np.random.uniform(0.0, 1.0, (C, P)))
    idx = np.concatenate([np.random.permutation(S)[:P] for _ in range(K)])
    return {"x": x, "ff": ff, "offs": striped(idx)}


def reference(x, ff, offs):
    idx = offs[:16].T.reshape(-1)
    neg = -f64(ff)
    d = f64(x)[:, idx].reshape(C, K, P) + neg[:, None, :]
    return np.abs(d).reshape(C, N)

@@ -1,0 +1,38 @@
+import concourse.mybir as mybir
+
+F32 = mybir.dt.float32
+U16 = mybir.dt.uint16
+ADD = mybir.AluOpType.add
+ABS = mybir.ActivationFunctionType.Abs
+
+CHANNELS = 128
+PIXELS = 1024
+FROM = 512
+PARTNERS = 4
+OFFSETS_PER_COLUMN = 16
+
+
+def tile_affinityhead_kernel(tc, x, ff, offs, out):
+    nc = tc.nc
+    piece_columns = FROM // OFFSETS_PER_COLUMN
+    with (
+        tc.tile_pool(name="held", bufs=1) as held,
+        tc.tile_pool(name="pieces", bufs=PARTNERS) as pieces,
+    ):
+        offsets = held.tile([CHANNELS, PARTNERS * piece_columns], U16, name="offsets")
+        nc.sync.dma_start(offsets[:], offs)
+        from_pixels = held.tile([CHANNELS, FROM], F32, name="from_pixels")
+        nc.scalar.dma_start(from_pixels[:], ff)
+        window = held.tile([CHANNELS, PIXELS], F32, name="window")
+        nc.sync.dma_start(window[:], x)
+
+        negated = held.tile([CHANNELS, FROM], F32, name="negated")
+        nc.scalar.mul(negated[:], from_pixels[:], -1.0)
+
+        for k in range(PARTNERS):
+            picked = window[:].indirect(offsets[:, k * piece_columns : (k + 1) * piece_columns])
+            difference = pieces.tile([CHANNELS, FROM], F32, name="difference")
+            nc.vector.tensor_tensor(difference[:], picked, negated[:], ADD)
+            distance = pieces.tile([CHANNELS, FROM], F32, name="distance")
+            nc.scalar.activation(distance[:], difference[:], ABS)
+            nc.sync.dma_start(out[:, k * FROM : (k + 1) * FROM], distance[:])

@@ -8,18 +8,30 @@ ABS = mybir.ActivationFunctionType.Abs
 CHANNELS = 128
 PIXELS = 1024
 FROM = 512
-PARTNERS = 4
+ENTRIES = 2048
 OFFSETS_PER_COLUMN = 16
+SMALLEST_PIECE = 256
+
+
+def shrinking_pieces(total, longest, smallest):
+    pieces = []
+    start = 0
+    while total - start > smallest:
+        length = min(longest, (total - start) // 2)
+        pieces.append((start, length))
+        start += length
+    pieces.append((start, total - start))
+    return pieces
 
 
 def tile_affinityhead_kernel(tc, x, ff, offs, out):
     nc = tc.nc
-    piece_columns = FROM // OFFSETS_PER_COLUMN
+    list_pieces = shrinking_pieces(ENTRIES, FROM, SMALLEST_PIECE)
     with (
         tc.tile_pool(name="held", bufs=1) as held,
-        tc.tile_pool(name="pieces", bufs=PARTNERS) as pieces,
+        tc.tile_pool(name="pieces", bufs=len(list_pieces)) as pieces,
     ):
-        offsets = held.tile([CHANNELS, PARTNERS * piece_columns], U16, name="offsets")
+        offsets = held.tile([CHANNELS, ENTRIES // OFFSETS_PER_COLUMN], U16, name="offsets")
         nc.sync.dma_start(offsets[:], offs)
         from_pixels = held.tile([CHANNELS, FROM], F32, name="from_pixels")
         nc.scalar.dma_start(from_pixels[:], ff)
@@ -29,10 +41,13 @@ def tile_affinityhead_kernel(tc, x, ff, offs, out):
         negated = held.tile([CHANNELS, FROM], F32, name="negated")
         nc.scalar.mul(negated[:], from_pixels[:], -1.0)
 
-        for k in range(PARTNERS):
-            picked = window[:].indirect(offsets[:, k * piece_columns : (k + 1) * piece_columns])
-            difference = pieces.tile([CHANNELS, FROM], F32, name="difference")
-            nc.vector.tensor_tensor(difference[:], picked, negated[:], ADD)
-            distance = pieces.tile([CHANNELS, FROM], F32, name="distance")
+        for start, length in list_pieces:
+            first = start % FROM
+            picked = window[:].indirect(
+                offsets[:, start // OFFSETS_PER_COLUMN : (start + length) // OFFSETS_PER_COLUMN]
+            )
+            difference = pieces.tile([CHANNELS, length], F32, name="difference")
+            nc.vector.tensor_tensor(difference[:], picked, negated[:, first : first + length], ADD)
+            distance = pieces.tile([CHANNELS, length], F32, name="distance")
             nc.scalar.activation(distance[:], difference[:], ABS)
-            nc.sync.dma_start(out[:, k * FROM : (k + 1) * FROM], distance[:])
+            nc.sync.dma_start(out[:, start : start + length], distance[:])

@@ -10,6 +10,7 @@ PIXELS = 1024
 FROM = 512
 ENTRIES = 2048
 OFFSETS_PER_COLUMN = 16
+COPIES = 2
 SMALLEST_PIECE = 256
 
 
@@ -26,7 +27,7 @@ def shrinking_pieces(total, longest, smallest):
 
 def tile_affinityhead_kernel(tc, x, ff, offs, out):
     nc = tc.nc
-    list_pieces = shrinking_pieces(ENTRIES, FROM, SMALLEST_PIECE)
+    list_pieces = shrinking_pieces(ENTRIES, COPIES * FROM, SMALLEST_PIECE)
     with (
         tc.tile_pool(name="held", bufs=1) as held,
         tc.tile_pool(name="pieces", bufs=len(list_pieces)) as pieces,
@@ -38,8 +39,9 @@ def tile_affinityhead_kernel(tc, x, ff, offs, out):
         window = held.tile([CHANNELS, PIXELS], F32, name="window")
         nc.sync.dma_start(window[:], x)
 
-        negated = held.tile([CHANNELS, FROM], F32, name="negated")
-        nc.scalar.mul(negated[:], from_pixels[:], -1.0)
+        negated = held.tile([CHANNELS, COPIES * FROM], F32, name="negated")
+        nc.scalar.mul(negated[:, :FROM], from_pixels[:], -1.0)
+        nc.vector.tensor_scalar_mul(negated[:, FROM:], from_pixels[:], -1.0)
 
         for start, length in list_pieces:
             first = start % FROM

@@ -10,7 +10,6 @@ PIXELS = 1024
 FROM = 512
 ENTRIES = 2048
 OFFSETS_PER_COLUMN = 16
-COPIES = 2
 SMALLEST_PIECE = 256
 
 
@@ -27,7 +26,7 @@ def shrinking_pieces(total, longest, smallest):
 
 def tile_affinityhead_kernel(tc, x, ff, offs, out):
     nc = tc.nc
-    list_pieces = shrinking_pieces(ENTRIES, COPIES * FROM, SMALLEST_PIECE)
+    list_pieces = shrinking_pieces(ENTRIES, FROM, SMALLEST_PIECE)
     with (
         tc.tile_pool(name="held", bufs=1) as held,
         tc.tile_pool(name="pieces", bufs=len(list_pieces)) as pieces,
@@ -39,9 +38,8 @@ def tile_affinityhead_kernel(tc, x, ff, offs, out):
         window = held.tile([CHANNELS, PIXELS], F32, name="window")
         nc.sync.dma_start(window[:], x)
 
-        negated = held.tile([CHANNELS, COPIES * FROM], F32, name="negated")
-        nc.scalar.mul(negated[:, :FROM], from_pixels[:], -1.0)
-        nc.vector.tensor_scalar_mul(negated[:, FROM:], from_pixels[:], -1.0)
+        negated = held.tile([CHANNELS, FROM], F32, name="negated")
+        nc.vector.tensor_scalar_mul(negated[:], from_pixels[:], -1.0)
 
         for start, length in list_pieces:
             first = start % FROM

@@ -8,46 +8,39 @@ ABS = mybir.ActivationFunctionType.Abs
 CHANNELS = 128
 PIXELS = 1024
 FROM = 512
-ENTRIES = 2048
+PARTNERS = 4
 OFFSETS_PER_COLUMN = 16
-SMALLEST_PIECE = 256
-
-
-def shrinking_pieces(total, longest, smallest):
-    pieces = []
-    start = 0
-    while total - start > smallest:
-        length = min(longest, (total - start) // 2)
-        pieces.append((start, length))
-        start += length
-    pieces.append((start, total - start))
-    return pieces
+HALF = FROM // 2
 
 
 def tile_affinityhead_kernel(tc, x, ff, offs, out):
     nc = tc.nc
-    list_pieces = shrinking_pieces(ENTRIES, FROM, SMALLEST_PIECE)
     with (
         tc.tile_pool(name="held", bufs=1) as held,
-        tc.tile_pool(name="pieces", bufs=len(list_pieces)) as pieces,
+        tc.tile_pool(name="pieces", bufs=2 * PARTNERS) as pieces,
     ):
-        offsets = held.tile([CHANNELS, ENTRIES // OFFSETS_PER_COLUMN], U16, name="offsets")
-        nc.sync.dma_start(offsets[:], offs)
         from_pixels = held.tile([CHANNELS, FROM], F32, name="from_pixels")
-        nc.scalar.dma_start(from_pixels[:], ff)
+        nc.sync.dma_start(from_pixels[:, :HALF], ff[:, :HALF])
+        offsets = held.tile([CHANNELS, PARTNERS * FROM // OFFSETS_PER_COLUMN], U16, name="offsets")
+        nc.sync.dma_start(offsets[:], offs)
         window = held.tile([CHANNELS, PIXELS], F32, name="window")
-        nc.sync.dma_start(window[:], x)
+        nc.scalar.dma_start(window[:], x)
+        nc.scalar.dma_start(from_pixels[:, HALF:], ff[:, HALF:])
 
         negated = held.tile([CHANNELS, FROM], F32, name="negated")
-        nc.vector.tensor_scalar_mul(negated[:], from_pixels[:], -1.0)
+        nc.vector.tensor_scalar_mul(negated[:, :HALF], from_pixels[:, :HALF], -1.0)
+        nc.scalar.mul(negated[:, HALF:], from_pixels[:, HALF:], -1.0)
 
-        for start, length in list_pieces:
-            first = start % FROM
-            picked = window[:].indirect(
-                offsets[:, start // OFFSETS_PER_COLUMN : (start + length) // OFFSETS_PER_COLUMN]
-            )
-            difference = pieces.tile([CHANNELS, length], F32, name="difference")
-            nc.vector.tensor_tensor(difference[:], picked, negated[:, first : first + length], ADD)
-            distance = pieces.tile([CHANNELS, length], F32, name="distance")
-            nc.scalar.activation(distance[:], difference[:], ABS)
-            nc.sync.dma_start(out[:, start : start + length], distance[:])
+        for first in (0, HALF):
+            for partner in range(PARTNERS):
+                start = partner * FROM + first
+                picked = window[:].indirect(
+                    offsets[:, start // OFFSETS_PER_COLUMN : (start + HALF) // OFFSETS_PER_COLUMN]
+                )
+                difference = pieces.tile([CHANNELS, HALF], F32, name="difference")
+                nc.vector.tensor_tensor(
+                    difference[:], picked, negated[:, first : first + HALF], ADD
+                )
+                distance = pieces.tile([CHANNELS, HALF], F32, name="distance")
+                nc.scalar.activation(distance[:], difference[:], ABS)
+                nc.sync.dma_start(out[:, start : start + HALF], distance[:])

@@ -10,7 +10,7 @@ PIXELS = 1024
 FROM = 512
 PARTNERS = 4
 OFFSETS_PER_COLUMN = 16
-HALF = FROM // 2
+EARLY = 128
 
 
 def tile_affinityhead_kernel(tc, x, ff, offs, out):
@@ -20,27 +20,27 @@ def tile_affinityhead_kernel(tc, x, ff, offs, out):
         tc.tile_pool(name="pieces", bufs=2 * PARTNERS) as pieces,
     ):
         from_pixels = held.tile([CHANNELS, FROM], F32, name="from_pixels")
-        nc.sync.dma_start(from_pixels[:, :HALF], ff[:, :HALF])
+        nc.sync.dma_start(from_pixels[:, :EARLY], ff[:, :EARLY])
         offsets = held.tile([CHANNELS, PARTNERS * FROM // OFFSETS_PER_COLUMN], U16, name="offsets")
         nc.sync.dma_start(offsets[:], offs)
         window = held.tile([CHANNELS, PIXELS], F32, name="window")
         nc.scalar.dma_start(window[:], x)
-        nc.scalar.dma_start(from_pixels[:, HALF:], ff[:, HALF:])
+        nc.scalar.dma_start(from_pixels[:, EARLY:], ff[:, EARLY:])
 
         negated = held.tile([CHANNELS, FROM], F32, name="negated")
-        nc.vector.tensor_scalar_mul(negated[:, :HALF], from_pixels[:, :HALF], -1.0)
-        nc.scalar.mul(negated[:, HALF:], from_pixels[:, HALF:], -1.0)
+        nc.vector.tensor_scalar_mul(negated[:, :EARLY], from_pixels[:, :EARLY], -1.0)
+        nc.scalar.mul(negated[:, EARLY:], from_pixels[:, EARLY:], -1.0)
 
-        for first in (0, HALF):
+        for first, width in ((0, EARLY), (EARLY, FROM - EARLY)):
             for partner in range(PARTNERS):
                 start = partner * FROM + first
                 picked = window[:].indirect(
-                    offsets[:, start // OFFSETS_PER_COLUMN : (start + HALF) // OFFSETS_PER_COLUMN]
+                    offsets[:, start // OFFSETS_PER_COLUMN : (start + width) // OFFSETS_PER_COLUMN]
                 )
-                difference = pieces.tile([CHANNELS, HALF], F32, name="difference")
+                difference = pieces.tile([CHANNELS, width], F32, name="difference")
                 nc.vector.tensor_tensor(
-                    difference[:], picked, negated[:, first : first + HALF], ADD
+                    difference[:], picked, negated[:, first : first + width], ADD
                 )
-                distance = pieces.tile([CHANNELS, HALF], F32, name="distance")
+                distance = pieces.tile([CHANNELS, width], F32, name="distance")
                 nc.scalar.activation(distance[:], difference[:], ABS)
-                nc.sync.dma_start(out[:, start : start + HALF], distance[:])
+                nc.sync.dma_start(out[:, start : start + width], distance[:])

@@ -11,13 +11,14 @@ FROM = 512
 PARTNERS = 4
 OFFSETS_PER_COLUMN = 16
 EARLY = 128
+BLOCKS = ((0, EARLY), (EARLY, FROM - 2 * EARLY), (FROM - EARLY, EARLY))
 
 
 def tile_affinityhead_kernel(tc, x, ff, offs, out):
     nc = tc.nc
     with (
         tc.tile_pool(name="held", bufs=1) as held,
-        tc.tile_pool(name="pieces", bufs=2 * PARTNERS) as pieces,
+        tc.tile_pool(name="pieces", bufs=len(BLOCKS) * PARTNERS) as pieces,
     ):
         from_pixels = held.tile([CHANNELS, FROM], F32, name="from_pixels")
         nc.sync.dma_start(from_pixels[:, :EARLY], ff[:, :EARLY])
@@ -31,7 +32,7 @@ def tile_affinityhead_kernel(tc, x, ff, offs, out):
         nc.vector.tensor_scalar_mul(negated[:, :EARLY], from_pixels[:, :EARLY], -1.0)
         nc.scalar.mul(negated[:, EARLY:], from_pixels[:, EARLY:], -1.0)
 
-        for first, width in ((0, EARLY), (EARLY, FROM - EARLY)):
+        for first, width in BLOCKS:
             for partner in range(PARTNERS):
                 start = partner * FROM + first
                 picked = window[:].indirect(

@@ -30,7 +30,10 @@ def tile_affinityhead_kernel(tc, x, ff, offs, out):
 
         negated = held.tile([CHANNELS, FROM], F32, name="negated")
         nc.vector.tensor_scalar_mul(negated[:, :EARLY], from_pixels[:, :EARLY], -1.0)
-        nc.scalar.mul(negated[:, EARLY:], from_pixels[:, EARLY:], -1.0)
+        for first, width in BLOCKS[1:]:
+            nc.scalar.mul(
+                negated[:, first : first + width], from_pixels[:, first : first + width], -1.0
+            )
 
         for first, width in BLOCKS:
             for partner in range(PARTNERS):

@@ -2,9 +2,12 @@ import concourse.mybir as mybir
 
 F32 = mybir.dt.float32
 U16 = mybir.dt.uint16
+I32 = mybir.dt.int32
 ADD = mybir.AluOpType.add
+BITWISE_AND = mybir.AluOpType.bitwise_and
 ABS = mybir.ActivationFunctionType.Abs
 
+ALL_BUT_SIGN = 0x7FFFFFFF
 CHANNELS = 128
 PIXELS = 1024
 FROM = 512
@@ -46,5 +49,10 @@ def tile_affinityhead_kernel(tc, x, ff, offs, out):
                     difference[:], picked, negated[:, first : first + width], ADD
                 )
                 distance = pieces.tile([CHANNELS, width], F32, name="distance")
-                nc.scalar.activation(distance[:], difference[:], ABS)
+                if start + width < PARTNERS * FROM:
+                    nc.scalar.activation(distance[:], difference[:], ABS)
+                else:
+                    nc.vector.tensor_single_scalar(
+                        distance[:].bitcast(I32), difference[:].bitcast(I32), ALL_BUT_SIGN, BITWISE_AND
+                    )
                 nc.sync.dma_start(out[:, start : start + width], distance[:])

@@ -41,18 +41,26 @@ def tile_affinityhead_kernel(tc, x, ff, offs, out):
         for first, width in BLOCKS:
             for partner in range(PARTNERS):
                 start = partner * FROM + first
-                picked = window[:].indirect(
-                    offsets[:, start // OFFSETS_PER_COLUMN : (start + width) // OFFSETS_PER_COLUMN]
-                )
+                last = start + width == PARTNERS * FROM
+                step = width // 2 if last else width
                 difference = pieces.tile([CHANNELS, width], F32, name="difference")
-                nc.vector.tensor_tensor(
-                    difference[:], picked, negated[:, first : first + width], ADD
-                )
                 distance = pieces.tile([CHANNELS, width], F32, name="distance")
-                if start + width < PARTNERS * FROM:
-                    nc.scalar.activation(distance[:], difference[:], ABS)
-                else:
-                    nc.vector.tensor_single_scalar(
-                        distance[:].bitcast(I32), difference[:].bitcast(I32), ALL_BUT_SIGN, BITWISE_AND
+                for at in range(0, width, step):
+                    entry = start + at
+                    columns = slice(at, at + step)
+                    picked = window[:].indirect(
+                        offsets[:, entry // OFFSETS_PER_COLUMN : (entry + step) // OFFSETS_PER_COLUMN]
                     )
+                    nc.vector.tensor_tensor(
+                        difference[:, columns], picked, negated[:, first + at : first + at + step], ADD
+                    )
+                    if last and at > 0:
+                        nc.vector.tensor_single_scalar(
+                            distance[:, columns].bitcast(I32),
+                            difference[:, columns].bitcast(I32),
+                            ALL_BUT_SIGN,
+                            BITWISE_AND,
+                        )
+                    else:
+                        nc.scalar.activation(distance[:, columns], difference[:, columns], ABS)
                 nc.sync.dma_start(out[:, start : start + width], distance[:])

import concourse.mybir as mybir

F32 = mybir.dt.float32
U16 = mybir.dt.uint16
I32 = mybir.dt.int32
ADD = mybir.AluOpType.add
BITWISE_AND = mybir.AluOpType.bitwise_and
ABS = mybir.ActivationFunctionType.Abs

ALL_BUT_SIGN = 0x7FFFFFFF
CHANNELS = 128
PIXELS = 1024
FROM = 512
PARTNERS = 4
OFFSETS_PER_COLUMN = 16
EARLY = 128
BLOCKS = ((0, EARLY), (EARLY, FROM - 2 * EARLY), (FROM - EARLY, EARLY))


def tile_affinityhead_kernel(tc, x, ff, offs, out):
    nc = tc.nc
    with (
        tc.tile_pool(name="held", bufs=1) as held,
        tc.tile_pool(name="pieces", bufs=len(BLOCKS) * PARTNERS) as pieces,
    ):
        from_pixels = held.tile([CHANNELS, FROM], F32, name="from_pixels")
        nc.sync.dma_start(from_pixels[:, :EARLY], ff[:, :EARLY])
        offsets = held.tile([CHANNELS, PARTNERS * FROM // OFFSETS_PER_COLUMN], U16, name="offsets")
        nc.sync.dma_start(offsets[:], offs)
        window = held.tile([CHANNELS, PIXELS], F32, name="window")
        nc.scalar.dma_start(window[:], x)
        nc.scalar.dma_start(from_pixels[:, EARLY:], ff[:, EARLY:])

        negated = held.tile([CHANNELS, FROM], F32, name="negated")
        nc.vector.tensor_scalar_mul(negated[:, :EARLY], from_pixels[:, :EARLY], -1.0)
        for first, width in BLOCKS[1:]:
            nc.scalar.mul(
                negated[:, first : first + width], from_pixels[:, first : first + width], -1.0
            )

        for first, width in BLOCKS:
            for partner in range(PARTNERS):
                start = partner * FROM + first
                last = start + width == PARTNERS * FROM
                step = width // 2 if last else width
                difference = pieces.tile([CHANNELS, width], F32, name="difference")
                distance = pieces.tile([CHANNELS, width], F32, name="distance")
                for at in range(0, width, step):
                    entry = start + at
                    columns = slice(at, at + step)
                    picked = window[:].indirect(
                        offsets[:, entry // OFFSETS_PER_COLUMN : (entry + step) // OFFSETS_PER_COLUMN]
                    )
                    nc.vector.tensor_tensor(
                        difference[:, columns], picked, negated[:, first + at : first + at + step], ADD
                    )
                    if last and at > 0:
                        nc.vector.tensor_single_scalar(
                            distance[:, columns].bitcast(I32),
                            difference[:, columns].bitcast(I32),
                            ALL_BUT_SIGN,
                            BITWISE_AND,
                        )
                    else:
                        nc.scalar.activation(distance[:, columns], difference[:, columns], ABS)
                nc.sync.dma_start(out[:, start : start + width], distance[:])
